import numpy as np
import ml_dtypes


def mxq(x, axis, fmt="e4m3"):
    dtype, down = {"e4m3": (ml_dtypes.float8_e4m3fn, 7), "e5m2": (ml_dtypes.float8_e5m2, 14)}[fmt]
    v = np.moveaxis(np.asarray(x, np.float32).astype(ml_dtypes.bfloat16).astype(np.float64), axis, -1)
    blocks = v.reshape(v.shape[:-1] + (-1, 32))
    amax = np.abs(blocks).max(-1, keepdims=True)
    byte = np.maximum(np.where(amax > 0, np.frexp(amax)[1] - 1 + 127, 0) - down, 1)
    scale = np.exp2(byte - 127.0)
    codes = (blocks / scale).astype(np.float32).astype(dtype).astype(np.float64)
    return np.moveaxis((codes * scale).reshape(v.shape), -1, axis)


WIDE = False


def mx_kscale(k):
    if not WIDE:
        return np.ones(k)
    levels = np.array([10, -10, 5, -5, 0])
    a = np.random.permutation(np.resize(levels, k // 512 * 4)).reshape(k // 512, 4)
    idx = np.arange(k)
    return np.exp2(a[idx // 512, idx % 128 // 32])


BF16 = ml_dtypes.bfloat16


def bf(x):
    return np.asarray(x, np.float32).astype(BF16)


def f64(x):
    return np.asarray(x).astype(np.float64)


E2M1 = np.array([0.0, 0.5, 1.0, 1.5, 2.0, 3.0, 4.0, 6.0, -0.0, -0.5, -1.0, -1.5, -2.0, -3.0, -4.0, -6.0])


def pack_weight(w, fmt):
    k, n = w.shape
    w = f64(bf(w)).reshape(k // 32, 32, n)
    amax = np.abs(w).max(1)
    if fmt == "e4m3":
        byte = np.frexp(amax)[1] - 1 + 127 - 7
    else:
        mant, ex = np.frexp(amax / 6.0)
        byte = np.where(mant > 0.5, ex, ex - 1) + 127
    byte = np.clip(np.where(amax > 0, byte, 1), 1, 254)
    scaled = (w * np.exp2(127.0 - byte)[:, None, :]).reshape(k, n).astype(np.float32)
    by_word = np.ascontiguousarray(scaled.reshape(k // 512, 128, 4, n).transpose(0, 1, 3, 2))
    if fmt == "e4m3":
        words = by_word.astype(ml_dtypes.float8_e4m3fn).view(np.uint8)
    else:
        c = by_word.astype(ml_dtypes.float4_e2m1fn).view(np.uint8) & 0xF
        words = c[..., 0::2] | (c[..., 1::2] << 4)
    return np.ascontiguousarray(words), np.ascontiguousarray(byte.astype(np.uint8).reshape(k // 512, 16, n))


def unpack_weight(words, scales, fmt):
    g, p, n, _ = words.shape
    if fmt == "e4m3":
        vals = np.ascontiguousarray(words).view(ml_dtypes.float8_e4m3fn).astype(np.float64)
    else:
        nib = np.empty((g, p, n, 4), np.uint8)
        nib[..., 0::2] = words & 0xF
        nib[..., 1::2] = words >> 4
        vals = E2M1[nib]
    vals = vals * np.repeat(np.exp2(scales.astype(np.float64) - 127.0), 8, axis=1)[..., None]
    return vals.transpose(0, 1, 3, 2).reshape(g * 512, n)


B, N, E, H, NOPE, VDIM, ROPE, QR, KVR = 4, 256, 2048, 16, 128, 128, 128, 512, 512
KVH = NOPE + VDIM
BASE = 10000.0
FMT = "e4m3"


def rope(v):
    d = v.shape[-1]
    n = v.shape[-2]
    theta = BASE ** (-2.0 * np.arange(d // 2) / d)
    ang = np.arange(n)[:, None] * theta[None, :]
    cos, sin = np.cos(ang), np.sin(ang)
    v1, v2 = v[..., 0::2], v[..., 1::2]
    return np.stack([v1 * cos - v2 * sin, v1 * sin + v2 * cos], axis=-1).reshape(v.shape)


def setup_inputs():
    s, t = mx_kscale(E), mx_kscale(KVR)
    tcol = np.concatenate([t, np.ones(ROPE)])
    x = bf(np.random.standard_normal((B, N, E)) * s)
    Wkva_words, Wkva_scales = pack_weight(np.random.standard_normal((E, KVR + ROPE)) / np.sqrt(E) / s[:, None] * tcol, FMT)
    Wkvb_words, Wkvb_scales = pack_weight(np.random.standard_normal((KVR, H * KVH)) / np.sqrt(KVR) / t[:, None], FMT)
    return {"x": x,
            "Wkva_words": Wkva_words, "Wkva_scales": Wkva_scales,
            "Wkvb_words": Wkvb_words, "Wkvb_scales": Wkvb_scales}


def reference(x, Wkva_words, Wkva_scales, Wkvb_words, Wkvb_scales):
    ckv = mxq(f64(x), 2, "e4m3") @ unpack_weight(Wkva_words, Wkva_scales, FMT)
    compressed, k_pe = ckv[..., :KVR], ckv[..., KVR:]
    k_pe = np.broadcast_to(k_pe[:, None], (B, H, N, ROPE))
    kv = mxq(compressed, 2, "e4m3") @ unpack_weight(Wkvb_words, Wkvb_scales, FMT)
    kv = kv.reshape(B, N, H, KVH).transpose(0, 2, 1, 3)
    k_nope, v = kv[..., :NOPE], kv[..., NOPE:]
    kf = np.concatenate([k_nope, rope(k_pe)], axis=-1)
    return kf, v

@@ -1,0 +1,304 @@
+import math
+from contextlib import ExitStack
+
+import concourse.mybir as mybir
+from concourse.masks import make_identity
+
+F32 = mybir.dt.float32
+BF16 = mybir.dt.bfloat16
+I32 = mybir.dt.int32
+U32 = mybir.dt.uint32
+U8 = mybir.dt.uint8
+FP8X4 = mybir.dt.float8_e4m3fn_x4
+ALU = mybir.AluOpType
+ACT = mybir.ActivationFunctionType
+
+P = 128
+PACK = 4
+K_PASS = P * PACK
+BATCH, POSITIONS, FEATURES = 4, 256, 2048
+HEADS, HEAD_DIM = 16, 128
+LATENT = 512
+X_PASSES = FEATURES // K_PASS
+CKV_COLS = LATENT + HEAD_DIM
+KV_COLS = HEADS * 2 * HEAD_DIM
+ROPE_BASE = 10000.0
+LOG2_HALF_DIM = 6
+HALF_DIM = 1 << LOG2_HALF_DIM
+
+LOG2_BATCHES_PER_PHASE = 1
+BATCHES_PER_PHASE = 1 << LOG2_BATCHES_PER_PHASE
+PHASES = BATCH // BATCHES_PER_PHASE
+TOK = POSITIONS * BATCHES_PER_PHASE // P
+TILES = PHASES * TOK
+PAIR_COLS = 512
+HEAD_PAIRS = KV_COLS // PAIR_COLS
+PAIRS_PER_ROUND = HEAD_PAIRS // TOK
+PLANES = 4
+WKVB_PLANE_COLS = KV_COLS // PLANES
+STAGE_BUFS = 6
+
+ROUND_MAGIC = 12582912.0
+TWO_PI_HIGH = 6.28125
+TWO_PI_LOW = 2.0 * math.pi - TWO_PI_HIGH
+
+FLOPS = 2 * BATCH * POSITIONS * (FEATURES * CKV_COLS + LATENT * KV_COLS)
+
+
+def tile_multilatentattention_pb_kernel(
+    tc, x, wkva_words, wkva_scales, wkvb_words, wkvb_scales, kf, v
+):
+    nc = tc.nc
+    with ExitStack() as ctx:
+        resident = ctx.enter_context(tc.tile_pool(name="resident", bufs=1))
+        work = ctx.enter_context(tc.tile_pool(name="work", bufs=2))
+        stage = ctx.enter_context(tc.tile_pool(name="stage", bufs=STAGE_BUFS))
+        psum_x = ctx.enter_context(tc.psum_pool(name="psum_x", bufs=2))
+        psum_c = ctx.enter_context(tc.psum_pool(name="psum_c", bufs=1))
+        psum_kv = ctx.enter_context(tc.psum_pool(name="psum_kv", bufs=3))
+
+        x_sb, c_codes, c_scales, rope = [], [], [], []
+        for ph in range(PHASES):
+            x_phase = resident.tile([P, TOK, FEATURES], BF16, name="x_phase%d" % ph)
+            x_sb.append(x_phase)
+            c_codes_phase = resident.tile([P, TOK, P], U32, name="c_codes%d" % ph, align_bytes=64)
+            c_codes.append(c_codes_phase)
+            c_scales_phase = resident.tile([P, TOK, P], U8, name="c_scales%d" % ph, align_bytes=64)
+            c_scales.append(c_scales_phase)
+            rope_phase = resident.tile([P, TOK, HEAD_DIM], F32, name="rope%d" % ph)
+            rope.append(rope_phase)
+        wkva = resident.tile([P, X_PASSES, CKV_COLS], U32, align_bytes=64)
+        wkvb = resident.tile([P, KV_COLS], U32, align_bytes=64)
+        wkva_planes = resident.tile([P, CKV_COLS], U8, align_bytes=64)
+        wkvb_planes = resident.tile([P, WKVB_PLANE_COLS], U8, align_bytes=64)
+        nc.vector.memset(wkva_planes[:].bitcast(I32), 0)
+        nc.vector.memset(wkvb_planes[:].bitcast(I32), 0)
+
+        def load_x(ph, e):
+            for b in range(BATCHES_PER_PHASE):
+                nc.sync.dma_start(
+                    out=x_sb[ph][b:P:BATCHES_PER_PHASE, e, :],
+                    in_=x[ph * BATCHES_PER_PHASE + b].rearrange("(q e) k -> e q k", e=TOK)[e],
+                )
+
+        load_x(0, 0)
+        for quadrant in range(4):
+            nc.sync.dma_start(
+                out=wkva_planes[32 * quadrant : 32 * quadrant + 4 * PLANES, :].bitcast(I32),
+                in_=wkva_scales[:, 4 * quadrant : 4 * quadrant + 4, :].bitcast(I32),
+            )
+        for g in range(X_PASSES):
+            nc.sync.dma_start(
+                out=wkva[:, g, :].bitcast(I32),
+                in_=wkva_words[g].rearrange("p n t -> p (n t)").bitcast(I32),
+            )
+        for e in range(1, TOK):
+            load_x(0, e)
+        for quadrant in range(4):
+            nc.sync.dma_start(
+                out=wkvb_planes[32 * quadrant : 32 * quadrant + 4 * PLANES, :].bitcast(I32),
+                in_=wkvb_scales[0, 4 * quadrant : 4 * quadrant + 4, :]
+                .rearrange("r (k n) -> k r n", k=PLANES)
+                .bitcast(I32),
+            )
+        wkvb_bytes = wkvb_words[0].rearrange("p n t -> p (n t)")
+        for k in range(PLANES):
+            first_col = WKVB_PLANE_COLS * k
+            nc.sync.dma_start(
+                out=wkvb[:, first_col : first_col + WKVB_PLANE_COLS].bitcast(I32),
+                in_=wkvb_bytes[:, PACK * first_col : PACK * (first_col + WKVB_PLANE_COLS)].bitcast(I32),
+            )
+        for ph in range(1, PHASES):
+            for e in range(TOK):
+                load_x(ph, e)
+
+        ident_f32 = resident.tile([P, P], F32)
+        make_identity(nc, ident_f32[:])
+        ident_bf16 = resident.tile([P, P], BF16)
+        make_identity(nc, ident_bf16[:])
+
+        partition_index = resident.tile([P, 1], I32)
+        nc.gpsimd.iota(partition_index[:], pattern=[[0, 1]], base=0, channel_multiplier=1)
+        offset_index = resident.tile([P, TOK], I32)
+        nc.gpsimd.iota(offset_index[:], pattern=[[1, TOK]], base=0, channel_multiplier=0)
+        row_index = resident.tile([P, 1], I32)
+        nc.vector.tensor_single_scalar(
+            out=row_index[:],
+            in_=partition_index[:],
+            scalar=LOG2_BATCHES_PER_PHASE,
+            op=ALU.arith_shift_right,
+        )
+        first_position = resident.tile([P, 1], F32)
+        nc.vector.tensor_scalar_mul(out=first_position[:], in0=row_index[:], scalar1=float(TOK))
+        position = resident.tile([P, TOK], F32)
+        nc.vector.tensor_scalar_add(out=position[:], in0=offset_index[:], scalar1=first_position[:, 0:1])
+
+        theta = resident.tile([P, HALF_DIM], F32)
+        nc.vector.memset(theta[:], 1.0)
+        for bit in range(LOG2_HALF_DIM):
+            span = 1 << bit
+            upper = theta[:].rearrange("p (hi two lo) -> p hi two lo", two=2, lo=span)[:, :, 1, :]
+            nc.vector.tensor_scalar_mul(out=upper, in0=upper, scalar1=ROPE_BASE ** (-span / HALF_DIM))
+
+        table_shape = [P, TOK, HALF_DIM]
+        angle = resident.tile([P, 2, TOK, HALF_DIM], F32)
+        nc.vector.tensor_tensor(
+            out=angle[:, 0],
+            in0=theta[:].unsqueeze(1).to_broadcast(table_shape),
+            in1=position[:].unsqueeze(2).to_broadcast(table_shape),
+            op=ALU.mult,
+        )
+        nc.vector.tensor_scalar_add(out=angle[:, 1], in0=angle[:, 0], scalar1=math.pi / 2.0)
+        angle_flat = angle[:].rearrange("p s e i -> p (s e i)")
+        turns = resident.tile([P, 2 * TOK * HALF_DIM], F32)
+        nc.vector.tensor_scalar(
+            out=turns[:],
+            in0=angle_flat,
+            scalar1=1.0 / (2.0 * math.pi),
+            scalar2=ROUND_MAGIC,
+            op0=ALU.mult,
+            op1=ALU.add,
+        )
+        nc.vector.tensor_scalar_sub(out=turns[:], in0=turns[:], scalar1=ROUND_MAGIC)
+        for part in (TWO_PI_HIGH, TWO_PI_LOW):
+            nc.vector.scalar_tensor_tensor(
+                out=angle_flat, in0=turns[:], scalar=-part, in1=angle_flat, op0=ALU.mult, op1=ALU.add
+            )
+        sin_cos = resident.tile([P, 2, TOK, HALF_DIM], F32)
+        nc.scalar.activation(out=sin_cos[:], in_=angle[:], func=ACT.Sin)
+        sin, cos = sin_cos[:, 0], sin_cos[:, 1]
+        minus_sin = resident.tile(table_shape, F32)
+        nc.vector.tensor_scalar_mul(out=minus_sin[:], in0=sin, scalar1=-1.0)
+
+        x_codes, x_scales, c_rounded = {}, {}, {}
+
+        def transpose_and_quantise_x(j):
+            ph, e = divmod(j, TOK)
+            words = x_sb[ph][:, e, :].bitcast(F32)
+            grouped = work.tile([P, X_PASSES, P, PACK], BF16, align_bytes=64)
+            grouped_words = grouped[:].bitcast(F32)
+            for half in range(2):
+                x_t = psum_x.tile([P, 2, 2, P], F32)
+                for gg in range(2):
+                    first_word = (2 * half + gg) * (K_PASS // 2)
+                    for u in range(2):
+                        nc.tensor.transpose(
+                            x_t[:, gg, u, :],
+                            words[:, first_word + u : first_word + K_PASS // 2 : 2],
+                            ident_f32[:],
+                        )
+                copy = nc.vector.tensor_copy if half == 0 else nc.scalar.copy
+                copy(
+                    out=grouped_words[:, 2 * half : 2 * half + 2],
+                    in_=x_t[:].rearrange("p g u r -> p g r u"),
+                )
+            codes = work.tile([P, X_PASSES, P], U32, align_bytes=64, bufs=3)
+            scales = work.tile([P, X_PASSES, P], U8, align_bytes=64, bufs=3)
+            nc.vector.quantize_mx(
+                out=codes[:].rearrange("p g r -> p (g r)").bitcast(FP8X4),
+                scales=scales[:].rearrange("p g r -> p (g r)"),
+                in_=grouped[:].rearrange("p g r t -> p (g r t)"),
+            )
+            x_codes[j], x_scales[j] = codes, scales
+
+        def rotate(k_pe, e, out):
+            pairs = k_pe.rearrange("p (i two) -> p i two", two=2)
+            straight = work.tile([P, HALF_DIM, 2], F32)
+            crossed = work.tile([P, HALF_DIM, 2], F32)
+            nc.vector.tensor_tensor(
+                out=straight[:],
+                in0=pairs,
+                in1=cos[:, e, :].unsqueeze(2).to_broadcast([P, HALF_DIM, 2]),
+                op=ALU.mult,
+            )
+            nc.vector.tensor_tensor(out=crossed[:, :, 0], in0=pairs[:, :, 1], in1=minus_sin[:, e, :], op=ALU.mult)
+            nc.vector.tensor_tensor(out=crossed[:, :, 1], in0=pairs[:, :, 0], in1=sin[:, e, :], op=ALU.mult)
+            nc.vector.tensor_tensor(
+                out=out,
+                in0=straight[:].rearrange("p i two -> p (i two)"),
+                in1=crossed[:].rearrange("p i two -> p (i two)"),
+                op=ALU.add,
+            )
+
+        def project_down(j):
+            ph, e = divmod(j, TOK)
+            c_acc = psum_c.tile([P, LATENT], F32)
+            k_pe = psum_c.tile([P, HEAD_DIM], F32)
+            for g in range(X_PASSES):
+                for acc, cols in ((c_acc, slice(0, LATENT)), (k_pe, slice(LATENT, CKV_COLS))):
+                    nc.tensor.matmul_mx(
+                        out=acc[:],
+                        lhsT=x_codes[j][:, g, :].bitcast(FP8X4),
+                        lhsT_scale=x_scales[j][:, g, :],
+                        rhs=wkva[:, g, cols].bitcast(FP8X4),
+                        rhs_scale=wkva_planes[4 * g : P, cols],
+                        start=(g == 0),
+                        stop=(g == X_PASSES - 1),
+                    )
+            c_bf16 = work.tile([P, PACK, P], BF16)
+            nc.scalar.copy(out=c_bf16[:], in_=c_acc[:].rearrange("p (i t) -> p t i", t=PACK))
+            c_rounded[j] = c_bf16
+            rotate(k_pe[:], e, rope[ph][:, e, :])
+
+        def transpose_and_quantise_c(j):
+            ph, e = divmod(j, TOK)
+            c_t = psum_c.tile([P, PACK, P], BF16)
+            for t in range(PACK):
+                nc.tensor.transpose(c_t[:, t, :], c_rounded[j][:, t, :], ident_bf16[:])
+            c_grouped = work.tile([P, P, PACK], BF16, align_bytes=64)
+            nc.scalar.copy(out=c_grouped[:], in_=c_t[:].rearrange("p t r -> p r t"))
+            nc.vector.quantize_mx(
+                out=c_codes[ph][:, e, :].bitcast(FP8X4),
+                scales=c_scales[ph][:, e, :],
+                in_=c_grouped[:].rearrange("p r t -> p (r t)"),
+            )
+
+        def project_up(ph, pair):
+            kf_stage = stage.tile([P, 2, TOK, 2 * HEAD_DIM], F32)
+            v_stage = stage.tile([P, 2, TOK, HEAD_DIM], F32)
+            nc.gpsimd.tensor_scalar(
+                out=kf_stage[:, :, :, HEAD_DIM:],
+                in0=rope[ph][:].unsqueeze(1).to_broadcast([P, 2, TOK, HEAD_DIM]),
+                scalar1=1.0,
+                scalar2=0.0,
+                op0=ALU.mult,
+                op1=ALU.add,
+            )
+            plane, plane_half = divmod(pair * PAIR_COLS, WKVB_PLANE_COLS)
+            for e in range(TOK):
+                kv = psum_kv.tile([P, 2, 2, HEAD_DIM], F32)
+                nc.tensor.matmul_mx(
+                    out=kv[:].rearrange("p h s d -> p (h s d)"),
+                    lhsT=c_codes[ph][:, e, :].bitcast(FP8X4),
+                    lhsT_scale=c_scales[ph][:, e, :],
+                    rhs=wkvb[:, pair * PAIR_COLS : (pair + 1) * PAIR_COLS].bitcast(FP8X4),
+                    rhs_scale=wkvb_planes[4 * plane : P, plane_half : plane_half + PAIR_COLS],
+                    start=True,
+                    stop=True,
+                )
+                copy = nc.vector.tensor_copy if e % 2 == 0 else nc.scalar.copy
+                copy(out=kf_stage[:, :, e, 0:HEAD_DIM], in_=kv[:, :, 0, :])
+                copy(out=v_stage[:, :, e, :], in_=kv[:, :, 1, :])
+            heads = slice(2 * pair, 2 * pair + 2)
+            for b in range(BATCHES_PER_PHASE):
+                batch = ph * BATCHES_PER_PHASE + b
+                nc.sync.dma_start(
+                    out=kf[batch, heads].rearrange("h (q e) d -> q h (e d)", e=TOK),
+                    in_=kf_stage[b:P:BATCHES_PER_PHASE].rearrange("p h e d -> p h (e d)"),
+                )
+                nc.sync.dma_start(
+                    out=v[batch, heads].rearrange("h (q e) d -> q h (e d)", e=TOK),
+                    in_=v_stage[b:P:BATCHES_PER_PHASE].rearrange("p h e d -> p h (e d)"),
+                )
+
+        for r in range(TILES + TOK + 1):
+            if r < TILES:
+                transpose_and_quantise_x(r)
+            if 0 <= r - 2 < TILES:
+                transpose_and_quantise_c(r - 2)
+            if 0 <= r - 1 < TILES:
+                project_down(r - 1)
+            if r > TOK:
+                ph, part = divmod(r - 1 - TOK, TOK)
+                for pair in range(part * PAIRS_PER_ROUND, (part + 1) * PAIRS_PER_ROUND):
+                    project_up(ph, pair)

@@ -26,17 +26,17 @@ ROPE_BASE = 10000.0
 LOG2_HALF_DIM = 6
 HALF_DIM = 1 << LOG2_HALF_DIM
 
-LOG2_BATCHES_PER_PHASE = 1
+LOG2_BATCHES_PER_PHASE = 0
 BATCHES_PER_PHASE = 1 << LOG2_BATCHES_PER_PHASE
 PHASES = BATCH // BATCHES_PER_PHASE
 TOK = POSITIONS * BATCHES_PER_PHASE // P
 TILES = PHASES * TOK
 PAIR_COLS = 512
 HEAD_PAIRS = KV_COLS // PAIR_COLS
-PAIRS_PER_ROUND = HEAD_PAIRS // TOK
+PAIRS_PER_TILE = HEAD_PAIRS // TOK
 PLANES = 4
 WKVB_PLANE_COLS = KV_COLS // PLANES
-STAGE_BUFS = 6
+STAGE_BUFS = 10
 
 ROUND_MAGIC = 12582912.0
 TWO_PI_HIGH = 6.28125
@@ -57,31 +57,39 @@ def tile_multilatentattention_pb_kernel(
         psum_c = ctx.enter_context(tc.psum_pool(name="psum_c", bufs=1))
         psum_kv = ctx.enter_context(tc.psum_pool(name="psum_kv", bufs=3))
 
-        x_sb, c_codes, c_scales, rope = [], [], [], []
+        x_sb = []
+        for j in range(TILES):
+            x_tile = resident.tile([P, FEATURES], BF16, name="x_tile%d" % j)
+            x_sb.append(x_tile)
+        c_codes, c_scales, rope = [], [], []
         for ph in range(PHASES):
-            x_phase = resident.tile([P, TOK, FEATURES], BF16, name="x_phase%d" % ph)
-            x_sb.append(x_phase)
             c_codes_phase = resident.tile([P, TOK, P], U32, name="c_codes%d" % ph, align_bytes=64)
             c_codes.append(c_codes_phase)
             c_scales_phase = resident.tile([P, TOK, P], U8, name="c_scales%d" % ph, align_bytes=64)
             c_scales.append(c_scales_phase)
             rope_phase = resident.tile([P, TOK, HEAD_DIM], F32, name="rope%d" % ph)
             rope.append(rope_phase)
-        wkva = resident.tile([P, X_PASSES, CKV_COLS], U32, align_bytes=64)
-        wkvb = resident.tile([P, KV_COLS], U32, align_bytes=64)
+        wkva, wkvb = [], []
+        for g in range(X_PASSES):
+            wkva_group = resident.tile([P, CKV_COLS], U32, name="wkva%d" % g, align_bytes=64)
+            wkva.append(wkva_group)
+        for k in range(PLANES):
+            wkvb_block = resident.tile([P, WKVB_PLANE_COLS], U32, name="wkvb%d" % k, align_bytes=64)
+            wkvb.append(wkvb_block)
         wkva_planes = resident.tile([P, CKV_COLS], U8, align_bytes=64)
         wkvb_planes = resident.tile([P, WKVB_PLANE_COLS], U8, align_bytes=64)
         nc.vector.memset(wkva_planes[:].bitcast(I32), 0)
         nc.vector.memset(wkvb_planes[:].bitcast(I32), 0)
 
-        def load_x(ph, e):
-            for b in range(BATCHES_PER_PHASE):
-                nc.sync.dma_start(
-                    out=x_sb[ph][b:P:BATCHES_PER_PHASE, e, :],
-                    in_=x[ph * BATCHES_PER_PHASE + b].rearrange("(q e) k -> e q k", e=TOK)[e],
-                )
+        def load_x(ph):
+            for e in range(TOK):
+                for b in range(BATCHES_PER_PHASE):
+                    nc.sync.dma_start(
+                        out=x_sb[ph * TOK + e][b:P:BATCHES_PER_PHASE, :],
+                        in_=x[ph * BATCHES_PER_PHASE + b].rearrange("(q e) k -> e q k", e=TOK)[e],
+                    )
 
-        load_x(0, 0)
+        load_x(0)
         for quadrant in range(4):
             nc.sync.dma_start(
                 out=wkva_planes[32 * quadrant : 32 * quadrant + 4 * PLANES, :].bitcast(I32),
@@ -89,11 +97,9 @@ def tile_multilatentattention_pb_kernel(
             )
         for g in range(X_PASSES):
             nc.sync.dma_start(
-                out=wkva[:, g, :].bitcast(I32),
+                out=wkva[g][:].bitcast(I32),
                 in_=wkva_words[g].rearrange("p n t -> p (n t)").bitcast(I32),
             )
-        for e in range(1, TOK):
-            load_x(0, e)
         for quadrant in range(4):
             nc.sync.dma_start(
                 out=wkvb_planes[32 * quadrant : 32 * quadrant + 4 * PLANES, :].bitcast(I32),
@@ -105,12 +111,11 @@ def tile_multilatentattention_pb_kernel(
         for k in range(PLANES):
             first_col = WKVB_PLANE_COLS * k
             nc.sync.dma_start(
-                out=wkvb[:, first_col : first_col + WKVB_PLANE_COLS].bitcast(I32),
+                out=wkvb[k][:].bitcast(I32),
                 in_=wkvb_bytes[:, PACK * first_col : PACK * (first_col + WKVB_PLANE_COLS)].bitcast(I32),
             )
         for ph in range(1, PHASES):
-            for e in range(TOK):
-                load_x(ph, e)
+            load_x(ph)
 
         ident_f32 = resident.tile([P, P], F32)
         make_identity(nc, ident_f32[:])
@@ -173,8 +178,7 @@ def tile_multilatentattention_pb_kernel(
         x_codes, x_scales, c_rounded = {}, {}, {}
 
         def transpose_and_quantise_x(j):
-            ph, e = divmod(j, TOK)
-            words = x_sb[ph][:, e, :].bitcast(F32)
+            words = x_sb[j][:].bitcast(F32)
             grouped = work.tile([P, X_PASSES, P, PACK], BF16, align_bytes=64)
             grouped_words = grouped[:].bitcast(F32)
             for half in range(2):
@@ -224,13 +228,13 @@ def tile_multilatentattention_pb_kernel(
             ph, e = divmod(j, TOK)
             c_acc = psum_c.tile([P, LATENT], F32)
             k_pe = psum_c.tile([P, HEAD_DIM], F32)
-            for g in range(X_PASSES):
-                for acc, cols in ((c_acc, slice(0, LATENT)), (k_pe, slice(LATENT, CKV_COLS))):
+            for acc, cols in ((c_acc, slice(0, LATENT)), (k_pe, slice(LATENT, CKV_COLS))):
+                for g in range(X_PASSES):
                     nc.tensor.matmul_mx(
                         out=acc[:],
                         lhsT=x_codes[j][:, g, :].bitcast(FP8X4),
                         lhsT_scale=x_scales[j][:, g, :],
-                        rhs=wkva[:, g, cols].bitcast(FP8X4),
+                        rhs=wkva[g][:, cols].bitcast(FP8X4),
                         rhs_scale=wkva_planes[4 * g : P, cols],
                         start=(g == 0),
                         stop=(g == X_PASSES - 1),
@@ -271,7 +275,7 @@ def tile_multilatentattention_pb_kernel(
                     out=kv[:].rearrange("p h s d -> p (h s d)"),
                     lhsT=c_codes[ph][:, e, :].bitcast(FP8X4),
                     lhsT_scale=c_scales[ph][:, e, :],
-                    rhs=wkvb[:, pair * PAIR_COLS : (pair + 1) * PAIR_COLS].bitcast(FP8X4),
+                    rhs=wkvb[plane][:, plane_half : plane_half + PAIR_COLS].bitcast(FP8X4),
                     rhs_scale=wkvb_planes[4 * plane : P, plane_half : plane_half + PAIR_COLS],
                     start=True,
                     stop=True,
@@ -291,14 +295,24 @@ def tile_multilatentattention_pb_kernel(
                     in_=v_stage[b:P:BATCHES_PER_PHASE].rearrange("p h e d -> p h (e d)"),
                 )
 
-        for r in range(TILES + TOK + 1):
-            if r < TILES:
-                transpose_and_quantise_x(r)
-            if 0 <= r - 2 < TILES:
-                transpose_and_quantise_c(r - 2)
-            if 0 <= r - 1 < TILES:
-                project_down(r - 1)
-            if r > TOK:
-                ph, part = divmod(r - 1 - TOK, TOK)
-                for pair in range(part * PAIRS_PER_ROUND, (part + 1) * PAIRS_PER_ROUND):
-                    project_up(ph, pair)
+        for s in range(TOK + 2):
+            if s < TOK:
+                transpose_and_quantise_x(s)
+            if 0 <= s - 2:
+                transpose_and_quantise_c(s - 2)
+            if 0 <= s - 1 < TOK:
+                project_down(s - 1)
+        for ph in range(PHASES):
+            for pair in range(HEAD_PAIRS):
+                project_up(ph, pair)
+                if ph + 1 < PHASES:
+                    e, step = divmod(pair, PAIRS_PER_TILE)
+                    j = (ph + 1) * TOK + e
+                    if step == 0:
+                        transpose_and_quantise_x(j)
+                        if e > 0:
+                            transpose_and_quantise_c(j - 1)
+                    if step == PAIRS_PER_TILE // 2:
+                        project_down(j)
+            if ph + 1 < PHASES:
+                transpose_and_quantise_c((ph + 2) * TOK - 1)

@@ -26,11 +26,7 @@ ROPE_BASE = 10000.0
 LOG2_HALF_DIM = 6
 HALF_DIM = 1 << LOG2_HALF_DIM
 
-LOG2_BATCHES_PER_PHASE = 0
-BATCHES_PER_PHASE = 1 << LOG2_BATCHES_PER_PHASE
-PHASES = BATCH // BATCHES_PER_PHASE
-TOK = POSITIONS * BATCHES_PER_PHASE // P
-TILES = PHASES * TOK
+TOK = POSITIONS // P
 PAIR_COLS = 512
 HEAD_PAIRS = KV_COLS // PAIR_COLS
 PAIRS_PER_TILE = HEAD_PAIRS // TOK
@@ -57,37 +53,28 @@ def tile_multilatentattention_pb_kernel(
         psum_c = ctx.enter_context(tc.psum_pool(name="psum_c", bufs=1))
         psum_kv = ctx.enter_context(tc.psum_pool(name="psum_kv", bufs=3))
 
-        x_sb = []
-        for j in range(TILES):
-            x_tile = resident.tile([P, FEATURES], BF16, name="x_tile%d" % j)
-            x_sb.append(x_tile)
-        c_codes, c_scales, rope = [], [], []
-        for ph in range(PHASES):
-            c_codes_phase = resident.tile([P, TOK, P], U32, name="c_codes%d" % ph, align_bytes=64)
-            c_codes.append(c_codes_phase)
-            c_scales_phase = resident.tile([P, TOK, P], U8, name="c_scales%d" % ph, align_bytes=64)
-            c_scales.append(c_scales_phase)
-            rope_phase = resident.tile([P, TOK, HEAD_DIM], F32, name="rope%d" % ph)
-            rope.append(rope_phase)
-        wkva, wkvb = [], []
-        for g in range(X_PASSES):
-            wkva_group = resident.tile([P, CKV_COLS], U32, name="wkva%d" % g, align_bytes=64)
-            wkva.append(wkva_group)
-        for k in range(PLANES):
-            wkvb_block = resident.tile([P, WKVB_PLANE_COLS], U32, name="wkvb%d" % k, align_bytes=64)
-            wkvb.append(wkvb_block)
+        x_sb, c_codes, c_scales, rope = [], [], [], []
+        for b in range(BATCH):
+            x_batch = resident.tile([P, TOK, FEATURES], BF16, name="x_batch%d" % b)
+            x_sb.append(x_batch)
+            c_codes_batch = resident.tile([P, TOK, P], U32, name="c_codes%d" % b, align_bytes=64)
+            c_codes.append(c_codes_batch)
+            c_scales_batch = resident.tile([P, TOK, P], U8, name="c_scales%d" % b, align_bytes=64)
+            c_scales.append(c_scales_batch)
+            rope_batch = resident.tile([P, TOK, HEAD_DIM], F32, name="rope%d" % b)
+            rope.append(rope_batch)
+        wkva = resident.tile([P, X_PASSES, CKV_COLS], U32, align_bytes=64)
+        wkvb = resident.tile([P, KV_COLS], U32, align_bytes=64)
         wkva_planes = resident.tile([P, CKV_COLS], U8, align_bytes=64)
         wkvb_planes = resident.tile([P, WKVB_PLANE_COLS], U8, align_bytes=64)
         nc.vector.memset(wkva_planes[:].bitcast(I32), 0)
         nc.vector.memset(wkvb_planes[:].bitcast(I32), 0)
 
-        def load_x(ph):
-            for e in range(TOK):
-                for b in range(BATCHES_PER_PHASE):
-                    nc.sync.dma_start(
-                        out=x_sb[ph * TOK + e][b:P:BATCHES_PER_PHASE, :],
-                        in_=x[ph * BATCHES_PER_PHASE + b].rearrange("(q e) k -> e q k", e=TOK)[e],
-                    )
+        def load_x(b):
+            nc.sync.dma_start(
+                out=x_sb[b][:].rearrange("p e k -> p (e k)"),
+                in_=x[b].rearrange("(p e) k -> p (e k)", e=TOK),
+            )
 
         load_x(0)
         for quadrant in range(4):
@@ -95,11 +82,10 @@ def tile_multilatentattention_pb_kernel(
                 out=wkva_planes[32 * quadrant : 32 * quadrant + 4 * PLANES, :].bitcast(I32),
                 in_=wkva_scales[:, 4 * quadrant : 4 * quadrant + 4, :].bitcast(I32),
             )
-        for g in range(X_PASSES):
-            nc.sync.dma_start(
-                out=wkva[g][:].bitcast(I32),
-                in_=wkva_words[g].rearrange("p n t -> p (n t)").bitcast(I32),
-            )
+        nc.sync.dma_start(
+            out=wkva[:].bitcast(I32),
+            in_=wkva_words.rearrange("g p n t -> p g (n t)").bitcast(I32),
+        )
         for quadrant in range(4):
             nc.sync.dma_start(
                 out=wkvb_planes[32 * quadrant : 32 * quadrant + 4 * PLANES, :].bitcast(I32),
@@ -107,36 +93,22 @@ def tile_multilatentattention_pb_kernel(
                 .rearrange("r (k n) -> k r n", k=PLANES)
                 .bitcast(I32),
             )
-        wkvb_bytes = wkvb_words[0].rearrange("p n t -> p (n t)")
-        for k in range(PLANES):
-            first_col = WKVB_PLANE_COLS * k
-            nc.sync.dma_start(
-                out=wkvb[k][:].bitcast(I32),
-                in_=wkvb_bytes[:, PACK * first_col : PACK * (first_col + WKVB_PLANE_COLS)].bitcast(I32),
-            )
-        for ph in range(1, PHASES):
-            load_x(ph)
+        nc.sync.dma_start(
+            out=wkvb[:].bitcast(I32),
+            in_=wkvb_words[0].rearrange("p n t -> p (n t)").bitcast(I32),
+        )
+        for b in range(1, BATCH):
+            load_x(b)
 
         ident_f32 = resident.tile([P, P], F32)
         make_identity(nc, ident_f32[:])
         ident_bf16 = resident.tile([P, P], BF16)
         make_identity(nc, ident_bf16[:])
 
-        partition_index = resident.tile([P, 1], I32)
-        nc.gpsimd.iota(partition_index[:], pattern=[[0, 1]], base=0, channel_multiplier=1)
-        offset_index = resident.tile([P, TOK], I32)
-        nc.gpsimd.iota(offset_index[:], pattern=[[1, TOK]], base=0, channel_multiplier=0)
-        row_index = resident.tile([P, 1], I32)
-        nc.vector.tensor_single_scalar(
-            out=row_index[:],
-            in_=partition_index[:],
-            scalar=LOG2_BATCHES_PER_PHASE,
-            op=ALU.arith_shift_right,
-        )
-        first_position = resident.tile([P, 1], F32)
-        nc.vector.tensor_scalar_mul(out=first_position[:], in0=row_index[:], scalar1=float(TOK))
+        position_index = resident.tile([P, TOK], I32)
+        nc.gpsimd.iota(position_index[:], pattern=[[1, TOK]], base=0, channel_multiplier=TOK)
         position = resident.tile([P, TOK], F32)
-        nc.vector.tensor_scalar_add(out=position[:], in0=offset_index[:], scalar1=first_position[:, 0:1])
+        nc.vector.tensor_copy(out=position[:], in_=position_index[:])
 
         theta = resident.tile([P, HALF_DIM], F32)
         nc.vector.memset(theta[:], 1.0)
@@ -177,8 +149,8 @@ def tile_multilatentattention_pb_kernel(
 
         x_codes, x_scales, c_rounded = {}, {}, {}
 
-        def transpose_and_quantise_x(j):
-            words = x_sb[j][:].bitcast(F32)
+        def transpose_and_quantise_x(b, e):
+            words = x_sb[b][:, e, :].bitcast(F32)
             grouped = work.tile([P, X_PASSES, P, PACK], BF16, align_bytes=64)
             grouped_words = grouped[:].bitcast(F32)
             for half in range(2):
@@ -203,7 +175,7 @@ def tile_multilatentattention_pb_kernel(
                 scales=scales[:].rearrange("p g r -> p (g r)"),
                 in_=grouped[:].rearrange("p g r t -> p (g r t)"),
             )
-            x_codes[j], x_scales[j] = codes, scales
+            x_codes[b, e], x_scales[b, e] = codes, scales
 
         def rotate(k_pe, e, out):
             pairs = k_pe.rearrange("p (i two) -> p i two", two=2)
@@ -224,59 +196,58 @@ def tile_multilatentattention_pb_kernel(
                 op=ALU.add,
             )
 
-        def project_down(j):
-            ph, e = divmod(j, TOK)
+        def project_down(b, e):
             c_acc = psum_c.tile([P, LATENT], F32)
             k_pe = psum_c.tile([P, HEAD_DIM], F32)
             for acc, cols in ((c_acc, slice(0, LATENT)), (k_pe, slice(LATENT, CKV_COLS))):
                 for g in range(X_PASSES):
                     nc.tensor.matmul_mx(
                         out=acc[:],
-                        lhsT=x_codes[j][:, g, :].bitcast(FP8X4),
-                        lhsT_scale=x_scales[j][:, g, :],
-                        rhs=wkva[g][:, cols].bitcast(FP8X4),
+                        lhsT=x_codes[b, e][:, g, :].bitcast(FP8X4),
+                        lhsT_scale=x_scales[b, e][:, g, :],
+                        rhs=wkva[:, g, cols].bitcast(FP8X4),
                         rhs_scale=wkva_planes[4 * g : P, cols],
                         start=(g == 0),
                         stop=(g == X_PASSES - 1),
                     )
             c_bf16 = work.tile([P, PACK, P], BF16)
             nc.scalar.copy(out=c_bf16[:], in_=c_acc[:].rearrange("p (i t) -> p t i", t=PACK))
-            c_rounded[j] = c_bf16
-            rotate(k_pe[:], e, rope[ph][:, e, :])
+            c_rounded[b, e] = c_bf16
+            rotate(k_pe[:], e, rope[b][:, e, :])
 
-        def transpose_and_quantise_c(j):
-            ph, e = divmod(j, TOK)
+        def transpose_and_quantise_c(b, e):
             c_t = psum_c.tile([P, PACK, P], BF16)
             for t in range(PACK):
-                nc.tensor.transpose(c_t[:, t, :], c_rounded[j][:, t, :], ident_bf16[:])
+                nc.tensor.transpose(c_t[:, t, :], c_rounded[b, e][:, t, :], ident_bf16[:])
             c_grouped = work.tile([P, P, PACK], BF16, align_bytes=64)
             nc.scalar.copy(out=c_grouped[:], in_=c_t[:].rearrange("p t r -> p r t"))
             nc.vector.quantize_mx(
-                out=c_codes[ph][:, e, :].bitcast(FP8X4),
-                scales=c_scales[ph][:, e, :],
+                out=c_codes[b][:, e, :].bitcast(FP8X4),
+                scales=c_scales[b][:, e, :],
                 in_=c_grouped[:].rearrange("p r t -> p (r t)"),
             )
 
-        def project_up(ph, pair):
+        def project_up(b, pair):
             kf_stage = stage.tile([P, 2, TOK, 2 * HEAD_DIM], F32)
             v_stage = stage.tile([P, 2, TOK, HEAD_DIM], F32)
             nc.gpsimd.tensor_scalar(
                 out=kf_stage[:, :, :, HEAD_DIM:],
-                in0=rope[ph][:].unsqueeze(1).to_broadcast([P, 2, TOK, HEAD_DIM]),
+                in0=rope[b][:].unsqueeze(1).to_broadcast([P, 2, TOK, HEAD_DIM]),
                 scalar1=1.0,
                 scalar2=0.0,
                 op0=ALU.mult,
                 op1=ALU.add,
             )
-            plane, plane_half = divmod(pair * PAIR_COLS, WKVB_PLANE_COLS)
+            cols = slice(pair * PAIR_COLS, (pair + 1) * PAIR_COLS)
+            plane, plane_col = divmod(pair * PAIR_COLS, WKVB_PLANE_COLS)
             for e in range(TOK):
                 kv = psum_kv.tile([P, 2, 2, HEAD_DIM], F32)
                 nc.tensor.matmul_mx(
                     out=kv[:].rearrange("p h s d -> p (h s d)"),
-                    lhsT=c_codes[ph][:, e, :].bitcast(FP8X4),
-                    lhsT_scale=c_scales[ph][:, e, :],
-                    rhs=wkvb[plane][:, plane_half : plane_half + PAIR_COLS].bitcast(FP8X4),
-                    rhs_scale=wkvb_planes[4 * plane : P, plane_half : plane_half + PAIR_COLS],
+                    lhsT=c_codes[b][:, e, :].bitcast(FP8X4),
+                    lhsT_scale=c_scales[b][:, e, :],
+                    rhs=wkvb[:, cols].bitcast(FP8X4),
+                    rhs_scale=wkvb_planes[4 * plane : P, plane_col : plane_col + PAIR_COLS],
                     start=True,
                     stop=True,
                 )
@@ -284,35 +255,27 @@ def tile_multilatentattention_pb_kernel(
                 copy(out=kf_stage[:, :, e, 0:HEAD_DIM], in_=kv[:, :, 0, :])
                 copy(out=v_stage[:, :, e, :], in_=kv[:, :, 1, :])
             heads = slice(2 * pair, 2 * pair + 2)
-            for b in range(BATCHES_PER_PHASE):
-                batch = ph * BATCHES_PER_PHASE + b
+            for out, staged in ((kf, kf_stage), (v, v_stage)):
                 nc.sync.dma_start(
-                    out=kf[batch, heads].rearrange("h (q e) d -> q h (e d)", e=TOK),
-                    in_=kf_stage[b:P:BATCHES_PER_PHASE].rearrange("p h e d -> p h (e d)"),
-                )
-                nc.sync.dma_start(
-                    out=v[batch, heads].rearrange("h (q e) d -> q h (e d)", e=TOK),
-                    in_=v_stage[b:P:BATCHES_PER_PHASE].rearrange("p h e d -> p h (e d)"),
+                    out=out[b, heads].rearrange("h (p e) d -> p h (e d)", e=TOK),
+                    in_=staged[:].rearrange("p h e d -> p h (e d)"),
                 )
 
-        for s in range(TOK + 2):
-            if s < TOK:
-                transpose_and_quantise_x(s)
-            if 0 <= s - 2:
-                transpose_and_quantise_c(s - 2)
-            if 0 <= s - 1 < TOK:
-                project_down(s - 1)
-        for ph in range(PHASES):
+        for e in range(TOK):
+            transpose_and_quantise_x(0, e)
+        for e in range(TOK):
+            project_down(0, e)
+            transpose_and_quantise_c(0, e)
+        for b in range(BATCH):
             for pair in range(HEAD_PAIRS):
-                project_up(ph, pair)
-                if ph + 1 < PHASES:
+                project_up(b, pair)
+                if b + 1 < BATCH:
                     e, step = divmod(pair, PAIRS_PER_TILE)
-                    j = (ph + 1) * TOK + e
                     if step == 0:
-                        transpose_and_quantise_x(j)
+                        transpose_and_quantise_x(b + 1, e)
                         if e > 0:
-                            transpose_and_quantise_c(j - 1)
+                            transpose_and_quantise_c(b + 1, e - 1)
                     if step == PAIRS_PER_TILE // 2:
-                        project_down(j)
-            if ph + 1 < PHASES:
-                transpose_and_quantise_c((ph + 2) * TOK - 1)
+                        project_down(b + 1, e)
+            if b + 1 < BATCH:
+                transpose_and_quantise_c(b + 1, TOK - 1)

@@ -53,28 +53,32 @@ def tile_multilatentattention_pb_kernel(
         psum_c = ctx.enter_context(tc.psum_pool(name="psum_c", bufs=1))
         psum_kv = ctx.enter_context(tc.psum_pool(name="psum_kv", bufs=3))
 
-        x_sb, c_codes, c_scales, rope = [], [], [], []
+        x_sb, c_codes, c_scales, rope = {}, [], [], []
         for b in range(BATCH):
-            x_batch = resident.tile([P, TOK, FEATURES], BF16, name="x_batch%d" % b)
-            x_sb.append(x_batch)
+            for e in range(TOK):
+                x_tile = resident.tile([P, FEATURES], BF16, name="x_tile%d_%d" % (b, e))
+                x_sb[b, e] = x_tile
             c_codes_batch = resident.tile([P, TOK, P], U32, name="c_codes%d" % b, align_bytes=64)
             c_codes.append(c_codes_batch)
             c_scales_batch = resident.tile([P, TOK, P], U8, name="c_scales%d" % b, align_bytes=64)
             c_scales.append(c_scales_batch)
             rope_batch = resident.tile([P, TOK, HEAD_DIM], F32, name="rope%d" % b)
             rope.append(rope_batch)
-        wkva = resident.tile([P, X_PASSES, CKV_COLS], U32, align_bytes=64)
-        wkvb = resident.tile([P, KV_COLS], U32, align_bytes=64)
+        wkva, wkvb = [], []
+        for g in range(X_PASSES):
+            wkva_group = resident.tile([P, CKV_COLS], U32, name="wkva%d" % g, align_bytes=64)
+            wkva.append(wkva_group)
+        for k in range(PLANES):
+            wkvb_block = resident.tile([P, WKVB_PLANE_COLS], U32, name="wkvb%d" % k, align_bytes=64)
+            wkvb.append(wkvb_block)
         wkva_planes = resident.tile([P, CKV_COLS], U8, align_bytes=64)
         wkvb_planes = resident.tile([P, WKVB_PLANE_COLS], U8, align_bytes=64)
         nc.vector.memset(wkva_planes[:].bitcast(I32), 0)
         nc.vector.memset(wkvb_planes[:].bitcast(I32), 0)
 
         def load_x(b):
-            nc.sync.dma_start(
-                out=x_sb[b][:].rearrange("p e k -> p (e k)"),
-                in_=x[b].rearrange("(p e) k -> p (e k)", e=TOK),
-            )
+            for e in range(TOK):
+                nc.sync.dma_start(out=x_sb[b, e][:], in_=x[b].rearrange("(p e) k -> e p k", e=TOK)[e])
 
         load_x(0)
         for quadrant in range(4):
@@ -82,10 +86,11 @@ def tile_multilatentattention_pb_kernel(
                 out=wkva_planes[32 * quadrant : 32 * quadrant + 4 * PLANES, :].bitcast(I32),
                 in_=wkva_scales[:, 4 * quadrant : 4 * quadrant + 4, :].bitcast(I32),
             )
-        nc.sync.dma_start(
-            out=wkva[:].bitcast(I32),
-            in_=wkva_words.rearrange("g p n t -> p g (n t)").bitcast(I32),
-        )
+        for g in range(X_PASSES):
+            nc.sync.dma_start(
+                out=wkva[g][:].bitcast(I32),
+                in_=wkva_words[g].rearrange("p n t -> p (n t)").bitcast(I32),
+            )
         for quadrant in range(4):
             nc.sync.dma_start(
                 out=wkvb_planes[32 * quadrant : 32 * quadrant + 4 * PLANES, :].bitcast(I32),
@@ -93,20 +98,22 @@ def tile_multilatentattention_pb_kernel(
                 .rearrange("r (k n) -> k r n", k=PLANES)
                 .bitcast(I32),
             )
-        nc.sync.dma_start(
-            out=wkvb[:].bitcast(I32),
-            in_=wkvb_words[0].rearrange("p n t -> p (n t)").bitcast(I32),
-        )
+        wkvb_bytes = wkvb_words[0].rearrange("p n t -> p (n t)")
+        for k in range(PLANES):
+            first_byte = PACK * WKVB_PLANE_COLS * k
+            nc.sync.dma_start(
+                out=wkvb[k][:].bitcast(I32),
+                in_=wkvb_bytes[:, first_byte : first_byte + PACK * WKVB_PLANE_COLS].bitcast(I32),
+            )
         for b in range(1, BATCH):
             load_x(b)
 
+        position_index = resident.tile([P, TOK], I32)
+        nc.gpsimd.iota(position_index[:], pattern=[[1, TOK]], base=0, channel_multiplier=TOK)
         ident_f32 = resident.tile([P, P], F32)
         make_identity(nc, ident_f32[:])
         ident_bf16 = resident.tile([P, P], BF16)
         make_identity(nc, ident_bf16[:])
-
-        position_index = resident.tile([P, TOK], I32)
-        nc.gpsimd.iota(position_index[:], pattern=[[1, TOK]], base=0, channel_multiplier=TOK)
         position = resident.tile([P, TOK], F32)
         nc.vector.tensor_copy(out=position[:], in_=position_index[:])
 
@@ -150,7 +157,7 @@ def tile_multilatentattention_pb_kernel(
         x_codes, x_scales, c_rounded = {}, {}, {}
 
         def transpose_and_quantise_x(b, e):
-            words = x_sb[b][:, e, :].bitcast(F32)
+            words = x_sb[b, e][:].bitcast(F32)
             grouped = work.tile([P, X_PASSES, P, PACK], BF16, align_bytes=64)
             grouped_words = grouped[:].bitcast(F32)
             for half in range(2):
@@ -205,7 +212,7 @@ def tile_multilatentattention_pb_kernel(
                         out=acc[:],
                         lhsT=x_codes[b, e][:, g, :].bitcast(FP8X4),
                         lhsT_scale=x_scales[b, e][:, g, :],
-                        rhs=wkva[:, g, cols].bitcast(FP8X4),
+                        rhs=wkva[g][:, cols].bitcast(FP8X4),
                         rhs_scale=wkva_planes[4 * g : P, cols],
                         start=(g == 0),
                         stop=(g == X_PASSES - 1),
@@ -238,16 +245,16 @@ def tile_multilatentattention_pb_kernel(
                 op0=ALU.mult,
                 op1=ALU.add,
             )
-            cols = slice(pair * PAIR_COLS, (pair + 1) * PAIR_COLS)
-            plane, plane_col = divmod(pair * PAIR_COLS, WKVB_PLANE_COLS)
+            plane, first_col = divmod(pair * PAIR_COLS, WKVB_PLANE_COLS)
+            cols = slice(first_col, first_col + PAIR_COLS)
             for e in range(TOK):
                 kv = psum_kv.tile([P, 2, 2, HEAD_DIM], F32)
                 nc.tensor.matmul_mx(
                     out=kv[:].rearrange("p h s d -> p (h s d)"),
                     lhsT=c_codes[b][:, e, :].bitcast(FP8X4),
                     lhsT_scale=c_scales[b][:, e, :],
-                    rhs=wkvb[:, cols].bitcast(FP8X4),
-                    rhs_scale=wkvb_planes[4 * plane : P, plane_col : plane_col + PAIR_COLS],
+                    rhs=wkvb[plane][:, cols].bitcast(FP8X4),
+                    rhs_scale=wkvb_planes[4 * plane : P, cols],
                     start=True,
                     stop=True,
                 )

@@ -29,7 +29,7 @@ HALF_DIM = 1 << LOG2_HALF_DIM
 TOK = POSITIONS // P
 PAIR_COLS = 512
 HEAD_PAIRS = KV_COLS // PAIR_COLS
-PAIRS_PER_TILE = HEAD_PAIRS // TOK
+NEXT_BATCH_STEPS = {0: (("x", 0),), 2: (("down", 0),), 3: (("x", 1), ("c", 0)), 5: (("down", 1),), 6: (("c", 1),)}
 PLANES = 4
 WKVB_PLANE_COLS = KV_COLS // PLANES
 STAGE_BUFS = 10
@@ -273,16 +273,10 @@ def tile_multilatentattention_pb_kernel(
         for e in range(TOK):
             project_down(0, e)
             transpose_and_quantise_c(0, e)
+        steps = {"x": transpose_and_quantise_x, "down": project_down, "c": transpose_and_quantise_c}
         for b in range(BATCH):
             for pair in range(HEAD_PAIRS):
                 project_up(b, pair)
                 if b + 1 < BATCH:
-                    e, step = divmod(pair, PAIRS_PER_TILE)
-                    if step == 0:
-                        transpose_and_quantise_x(b + 1, e)
-                        if e > 0:
-                            transpose_and_quantise_c(b + 1, e - 1)
-                    if step == PAIRS_PER_TILE // 2:
-                        project_down(b + 1, e)
-            if b + 1 < BATCH:
-                transpose_and_quantise_c(b + 1, TOK - 1)
+                    for step, e in NEXT_BATCH_STEPS.get(pair, ()):
+                        steps[step](b + 1, e)

@@ -30,6 +30,7 @@ TOK = POSITIONS // P
 PAIR_COLS = 512
 HEAD_PAIRS = KV_COLS // PAIR_COLS
 NEXT_BATCH_STEPS = {0: (("x", 0),), 2: (("down", 0),), 3: (("x", 1), ("c", 0)), 5: (("down", 1),), 6: (("c", 1),)}
+SECOND_BATCH_STEPS = {3: (("x", 0),), 4: (("x", 1),), 5: (("down", 0),), 6: (("down", 1), ("c", 0)), 7: (("c", 1),)}
 PLANES = 4
 WKVB_PLANE_COLS = KV_COLS // PLANES
 STAGE_BUFS = 10
@@ -278,5 +279,5 @@ def tile_multilatentattention_pb_kernel(
             for pair in range(HEAD_PAIRS):
                 project_up(b, pair)
                 if b + 1 < BATCH:
-                    for step, e in NEXT_BATCH_STEPS.get(pair, ()):
+                    for step, e in (SECOND_BATCH_STEPS if b == 0 else NEXT_BATCH_STEPS).get(pair, ()):
                         steps[step](b + 1, e)

import math
from contextlib import ExitStack

import concourse.mybir as mybir
from concourse.masks import make_identity

F32 = mybir.dt.float32
BF16 = mybir.dt.bfloat16
I32 = mybir.dt.int32
U32 = mybir.dt.uint32
U8 = mybir.dt.uint8
FP8X4 = mybir.dt.float8_e4m3fn_x4
ALU = mybir.AluOpType
ACT = mybir.ActivationFunctionType

P = 128
PACK = 4
K_PASS = P * PACK
BATCH, POSITIONS, FEATURES = 4, 256, 2048
HEADS, HEAD_DIM = 16, 128
LATENT = 512
X_PASSES = FEATURES // K_PASS
CKV_COLS = LATENT + HEAD_DIM
KV_COLS = HEADS * 2 * HEAD_DIM
ROPE_BASE = 10000.0
LOG2_HALF_DIM = 6
HALF_DIM = 1 << LOG2_HALF_DIM

TOK = POSITIONS // P
PAIR_COLS = 512
HEAD_PAIRS = KV_COLS // PAIR_COLS
NEXT_BATCH_STEPS = {0: (("x", 0),), 2: (("down", 0),), 3: (("x", 1), ("c", 0)), 5: (("down", 1),), 6: (("c", 1),)}
SECOND_BATCH_STEPS = {3: (("x", 0),), 4: (("x", 1),), 5: (("down", 0),), 6: (("down", 1), ("c", 0)), 7: (("c", 1),)}
PLANES = 4
WKVB_PLANE_COLS = KV_COLS // PLANES
STAGE_BUFS = 10

ROUND_MAGIC = 12582912.0
TWO_PI_HIGH = 6.28125
TWO_PI_LOW = 2.0 * math.pi - TWO_PI_HIGH

FLOPS = 2 * BATCH * POSITIONS * (FEATURES * CKV_COLS + LATENT * KV_COLS)


def tile_multilatentattention_pb_kernel(
    tc, x, wkva_words, wkva_scales, wkvb_words, wkvb_scales, kf, v
):
    nc = tc.nc
    with ExitStack() as ctx:
        resident = ctx.enter_context(tc.tile_pool(name="resident", bufs=1))
        work = ctx.enter_context(tc.tile_pool(name="work", bufs=2))
        stage = ctx.enter_context(tc.tile_pool(name="stage", bufs=STAGE_BUFS))
        psum_x = ctx.enter_context(tc.psum_pool(name="psum_x", bufs=2))
        psum_c = ctx.enter_context(tc.psum_pool(name="psum_c", bufs=1))
        psum_kv = ctx.enter_context(tc.psum_pool(name="psum_kv", bufs=3))

        x_sb, c_codes, c_scales, rope = {}, [], [], []
        for b in range(BATCH):
            for e in range(TOK):
                x_tile = resident.tile([P, FEATURES], BF16, name="x_tile%d_%d" % (b, e))
                x_sb[b, e] = x_tile
            c_codes_batch = resident.tile([P, TOK, P], U32, name="c_codes%d" % b, align_bytes=64)
            c_codes.append(c_codes_batch)
            c_scales_batch = resident.tile([P, TOK, P], U8, name="c_scales%d" % b, align_bytes=64)
            c_scales.append(c_scales_batch)
            rope_batch = resident.tile([P, TOK, HEAD_DIM], F32, name="rope%d" % b)
            rope.append(rope_batch)
        wkva, wkvb = [], []
        for g in range(X_PASSES):
            wkva_group = resident.tile([P, CKV_COLS], U32, name="wkva%d" % g, align_bytes=64)
            wkva.append(wkva_group)
        for k in range(PLANES):
            wkvb_block = resident.tile([P, WKVB_PLANE_COLS], U32, name="wkvb%d" % k, align_bytes=64)
            wkvb.append(wkvb_block)
        wkva_planes = resident.tile([P, CKV_COLS], U8, align_bytes=64)
        wkvb_planes = resident.tile([P, WKVB_PLANE_COLS], U8, align_bytes=64)
        nc.vector.memset(wkva_planes[:].bitcast(I32), 0)
        nc.vector.memset(wkvb_planes[:].bitcast(I32), 0)

        def load_x(b):
            for e in range(TOK):
                nc.sync.dma_start(out=x_sb[b, e][:], in_=x[b].rearrange("(p e) k -> e p k", e=TOK)[e])

        load_x(0)
        for quadrant in range(4):
            nc.sync.dma_start(
                out=wkva_planes[32 * quadrant : 32 * quadrant + 4 * PLANES, :].bitcast(I32),
                in_=wkva_scales[:, 4 * quadrant : 4 * quadrant + 4, :].bitcast(I32),
            )
        for g in range(X_PASSES):
            nc.sync.dma_start(
                out=wkva[g][:].bitcast(I32),
                in_=wkva_words[g].rearrange("p n t -> p (n t)").bitcast(I32),
            )
        for quadrant in range(4):
            nc.sync.dma_start(
                out=wkvb_planes[32 * quadrant : 32 * quadrant + 4 * PLANES, :].bitcast(I32),
                in_=wkvb_scales[0, 4 * quadrant : 4 * quadrant + 4, :]
                .rearrange("r (k n) -> k r n", k=PLANES)
                .bitcast(I32),
            )
        wkvb_bytes = wkvb_words[0].rearrange("p n t -> p (n t)")
        for k in range(PLANES):
            first_byte = PACK * WKVB_PLANE_COLS * k
            nc.sync.dma_start(
                out=wkvb[k][:].bitcast(I32),
                in_=wkvb_bytes[:, first_byte : first_byte + PACK * WKVB_PLANE_COLS].bitcast(I32),
            )
        for b in range(1, BATCH):
            load_x(b)

        position_index = resident.tile([P, TOK], I32)
        nc.gpsimd.iota(position_index[:], pattern=[[1, TOK]], base=0, channel_multiplier=TOK)
        ident_f32 = resident.tile([P, P], F32)
        make_identity(nc, ident_f32[:])
        ident_bf16 = resident.tile([P, P], BF16)
        make_identity(nc, ident_bf16[:])
        position = resident.tile([P, TOK], F32)
        nc.vector.tensor_copy(out=position[:], in_=position_index[:])

        theta = resident.tile([P, HALF_DIM], F32)
        nc.vector.memset(theta[:], 1.0)
        for bit in range(LOG2_HALF_DIM):
            span = 1 << bit
            upper = theta[:].rearrange("p (hi two lo) -> p hi two lo", two=2, lo=span)[:, :, 1, :]
            nc.vector.tensor_scalar_mul(out=upper, in0=upper, scalar1=ROPE_BASE ** (-span / HALF_DIM))

        table_shape = [P, TOK, HALF_DIM]
        angle = resident.tile([P, 2, TOK, HALF_DIM], F32)
        nc.vector.tensor_tensor(
            out=angle[:, 0],
            in0=theta[:].unsqueeze(1).to_broadcast(table_shape),
            in1=position[:].unsqueeze(2).to_broadcast(table_shape),
            op=ALU.mult,
        )
        nc.vector.tensor_scalar_add(out=angle[:, 1], in0=angle[:, 0], scalar1=math.pi / 2.0)
        angle_flat = angle[:].rearrange("p s e i -> p (s e i)")
        turns = resident.tile([P, 2 * TOK * HALF_DIM], F32)
        nc.vector.tensor_scalar(
            out=turns[:],
            in0=angle_flat,
            scalar1=1.0 / (2.0 * math.pi),
            scalar2=ROUND_MAGIC,
            op0=ALU.mult,
            op1=ALU.add,
        )
        nc.vector.tensor_scalar_sub(out=turns[:], in0=turns[:], scalar1=ROUND_MAGIC)
        for part in (TWO_PI_HIGH, TWO_PI_LOW):
            nc.vector.scalar_tensor_tensor(
                out=angle_flat, in0=turns[:], scalar=-part, in1=angle_flat, op0=ALU.mult, op1=ALU.add
            )
        sin_cos = resident.tile([P, 2, TOK, HALF_DIM], F32)
        nc.scalar.activation(out=sin_cos[:], in_=angle[:], func=ACT.Sin)
        sin, cos = sin_cos[:, 0], sin_cos[:, 1]
        minus_sin = resident.tile(table_shape, F32)
        nc.vector.tensor_scalar_mul(out=minus_sin[:], in0=sin, scalar1=-1.0)

        x_codes, x_scales, c_rounded = {}, {}, {}

        def transpose_and_quantise_x(b, e):
            words = x_sb[b, e][:].bitcast(F32)
            grouped = work.tile([P, X_PASSES, P, PACK], BF16, align_bytes=64)
            grouped_words = grouped[:].bitcast(F32)
            for half in range(2):
                x_t = psum_x.tile([P, 2, 2, P], F32)
                for gg in range(2):
                    first_word = (2 * half + gg) * (K_PASS // 2)
                    for u in range(2):
                        nc.tensor.transpose(
                            x_t[:, gg, u, :],
                            words[:, first_word + u : first_word + K_PASS // 2 : 2],
                            ident_f32[:],
                        )
                copy = nc.vector.tensor_copy if half == 0 else nc.scalar.copy
                copy(
                    out=grouped_words[:, 2 * half : 2 * half + 2],
                    in_=x_t[:].rearrange("p g u r -> p g r u"),
                )
            codes = work.tile([P, X_PASSES, P], U32, align_bytes=64, bufs=3)
            scales = work.tile([P, X_PASSES, P], U8, align_bytes=64, bufs=3)
            nc.vector.quantize_mx(
                out=codes[:].rearrange("p g r -> p (g r)").bitcast(FP8X4),
                scales=scales[:].rearrange("p g r -> p (g r)"),
                in_=grouped[:].rearrange("p g r t -> p (g r t)"),
            )
            x_codes[b, e], x_scales[b, e] = codes, scales

        def rotate(k_pe, e, out):
            pairs = k_pe.rearrange("p (i two) -> p i two", two=2)
            straight = work.tile([P, HALF_DIM, 2], F32)
            crossed = work.tile([P, HALF_DIM, 2], F32)
            nc.vector.tensor_tensor(
                out=straight[:],
                in0=pairs,
                in1=cos[:, e, :].unsqueeze(2).to_broadcast([P, HALF_DIM, 2]),
                op=ALU.mult,
            )
            nc.vector.tensor_tensor(out=crossed[:, :, 0], in0=pairs[:, :, 1], in1=minus_sin[:, e, :], op=ALU.mult)
            nc.vector.tensor_tensor(out=crossed[:, :, 1], in0=pairs[:, :, 0], in1=sin[:, e, :], op=ALU.mult)
            nc.vector.tensor_tensor(
                out=out,
                in0=straight[:].rearrange("p i two -> p (i two)"),
                in1=crossed[:].rearrange("p i two -> p (i two)"),
                op=ALU.add,
            )

        def project_down(b, e):
            c_acc = psum_c.tile([P, LATENT], F32)
            k_pe = psum_c.tile([P, HEAD_DIM], F32)
            for acc, cols in ((c_acc, slice(0, LATENT)), (k_pe, slice(LATENT, CKV_COLS))):
                for g in range(X_PASSES):
                    nc.tensor.matmul_mx(
                        out=acc[:],
                        lhsT=x_codes[b, e][:, g, :].bitcast(FP8X4),
                        lhsT_scale=x_scales[b, e][:, g, :],
                        rhs=wkva[g][:, cols].bitcast(FP8X4),
                        rhs_scale=wkva_planes[4 * g : P, cols],
                        start=(g == 0),
                        stop=(g == X_PASSES - 1),
                    )
            c_bf16 = work.tile([P, PACK, P], BF16)
            nc.scalar.copy(out=c_bf16[:], in_=c_acc[:].rearrange("p (i t) -> p t i", t=PACK))
            c_rounded[b, e] = c_bf16
            rotate(k_pe[:], e, rope[b][:, e, :])

        def transpose_and_quantise_c(b, e):
            c_t = psum_c.tile([P, PACK, P], BF16)
            for t in range(PACK):
                nc.tensor.transpose(c_t[:, t, :], c_rounded[b, e][:, t, :], ident_bf16[:])
            c_grouped = work.tile([P, P, PACK], BF16, align_bytes=64)
            nc.scalar.copy(out=c_grouped[:], in_=c_t[:].rearrange("p t r -> p r t"))
            nc.vector.quantize_mx(
                out=c_codes[b][:, e, :].bitcast(FP8X4),
                scales=c_scales[b][:, e, :],
                in_=c_grouped[:].rearrange("p r t -> p (r t)"),
            )

        def project_up(b, pair):
            kf_stage = stage.tile([P, 2, TOK, 2 * HEAD_DIM], F32)
            v_stage = stage.tile([P, 2, TOK, HEAD_DIM], F32)
            nc.gpsimd.tensor_scalar(
                out=kf_stage[:, :, :, HEAD_DIM:],
                in0=rope[b][:].unsqueeze(1).to_broadcast([P, 2, TOK, HEAD_DIM]),
                scalar1=1.0,
                scalar2=0.0,
                op0=ALU.mult,
                op1=ALU.add,
            )
            plane, first_col = divmod(pair * PAIR_COLS, WKVB_PLANE_COLS)
            cols = slice(first_col, first_col + PAIR_COLS)
            for e in range(TOK):
                kv = psum_kv.tile([P, 2, 2, HEAD_DIM], F32)
                nc.tensor.matmul_mx(
                    out=kv[:].rearrange("p h s d -> p (h s d)"),
                    lhsT=c_codes[b][:, e, :].bitcast(FP8X4),
                    lhsT_scale=c_scales[b][:, e, :],
                    rhs=wkvb[plane][:, cols].bitcast(FP8X4),
                    rhs_scale=wkvb_planes[4 * plane : P, cols],
                    start=True,
                    stop=True,
                )
                copy = nc.vector.tensor_copy if e % 2 == 0 else nc.scalar.copy
                copy(out=kf_stage[:, :, e, 0:HEAD_DIM], in_=kv[:, :, 0, :])
                copy(out=v_stage[:, :, e, :], in_=kv[:, :, 1, :])
            heads = slice(2 * pair, 2 * pair + 2)
            for out, staged in ((kf, kf_stage), (v, v_stage)):
                nc.sync.dma_start(
                    out=out[b, heads].rearrange("h (p e) d -> p h (e d)", e=TOK),
                    in_=staged[:].rearrange("p h e d -> p h (e d)"),
                )

        for e in range(TOK):
            transpose_and_quantise_x(0, e)
        for e in range(TOK):
            project_down(0, e)
            transpose_and_quantise_c(0, e)
        steps = {"x": transpose_and_quantise_x, "down": project_down, "c": transpose_and_quantise_c}
        for b in range(BATCH):
            for pair in range(HEAD_PAIRS):
                project_up(b, pair)
                if b + 1 < BATCH:
                    for step, e in (SECOND_BATCH_STEPS if b == 0 else NEXT_BATCH_STEPS).get(pair, ()):
                        steps[step](b + 1, e)
